import numpy as np
import ml_dtypes


def mxq(x, axis, fmt="e4m3"):
    dtype, down = {"e4m3": (ml_dtypes.float8_e4m3fn, 7), "e5m2": (ml_dtypes.float8_e5m2, 14)}[fmt]
    v = np.moveaxis(np.asarray(x, np.float32).astype(ml_dtypes.bfloat16).astype(np.float64), axis, -1)
    blocks = v.reshape(v.shape[:-1] + (-1, 32))
    amax = np.abs(blocks).max(-1, keepdims=True)
    byte = np.maximum(np.where(amax > 0, np.frexp(amax)[1] - 1 + 127, 0) - down, 1)
    scale = np.exp2(byte - 127.0)
    codes = (blocks / scale).astype(np.float32).astype(dtype).astype(np.float64)
    return np.moveaxis((codes * scale).reshape(v.shape), -1, axis)


WIDE = False


def mx_kscale(k):
    if not WIDE:
        return np.ones(k)
    levels = np.array([10, -10, 5, -5, 0])
    a = np.random.permutation(np.resize(levels, k // 512 * 4)).reshape(k // 512, 4)
    idx = np.arange(k)
    return np.exp2(a[idx // 512, idx % 128 // 32])


BF16 = ml_dtypes.bfloat16


def bf(x):
    return np.asarray(x, np.float32).astype(BF16)


def f64(x):
    return np.asarray(x).astype(np.float64)


B, S, D, H = 2, 64, 512, 1024
HEAD = H // 2


def rotate_every_two(x):
    x1 = x[..., ::2]
    x2 = x[..., 1::2]
    return np.stack((-x2, x1), axis=-1).reshape(x.shape)


def rope_table(seq_len):
    pos = np.arange(seq_len, dtype=np.float64)
    inv = 10000.0 ** (np.arange(0, HEAD, 2, dtype=np.float64) / HEAD)
    radians = pos[:, None] / inv
    sincos = np.stack((np.sin(radians), np.cos(radians)), axis=-1).reshape(seq_len, -1)
    return np.repeat(sincos, 2, axis=-1)


def setup_inputs():
    s = mx_kscale(D)
    u = np.repeat(mx_kscale(HEAD), 2)
    return {"hidden_states": bf(np.random.standard_normal((B, S, D)) * s),
            "Wq": bf(np.random.standard_normal((H, D)) / np.sqrt(D) / s * u[:, None]),
            "bq": bf(np.random.standard_normal(H) * 0.3 * u),
            "Wk": bf(np.random.standard_normal((H, D)) / np.sqrt(D) / s / u[:, None]),
            "bk": bf(np.random.standard_normal(H) * 0.3 / u)}


def reference(hidden_states, Wq, bq, Wk, bk):
    t = rope_table(hidden_states.shape[1])
    xq = mxq(f64(hidden_states), 2, "e4m3")
    q = (xq @ mxq(f64(Wq), 1, "e4m3").T) + f64(bq)
    k = (xq @ mxq(f64(Wk), 1, "e4m3").T) + f64(bk)
    q = q * t + rotate_every_two(q) * t
    k = k * t + rotate_every_two(k) * t
    return (mxq(q, 2, "e4m3") @ mxq(k, 2, "e4m3").transpose(0, 2, 1)) / np.sqrt(HEAD)

@@ -1,0 +1,245 @@
+import math
+from contextlib import ExitStack
+
+import concourse.mybir as mybir
+from concourse.masks import make_identity
+
+F32 = mybir.dt.float32
+BF16 = mybir.dt.bfloat16
+U32 = mybir.dt.uint32
+U8 = mybir.dt.uint8
+FP8X4 = mybir.dt.float8_e4m3fn_x4
+ALU = mybir.AluOpType
+ACT = mybir.ActivationFunctionType
+
+P = 128
+PACK = 4
+K_PASS = P * PACK
+
+BATCH, SEQ, D_IN, D_OUT = 2, 64, 512, 1024
+TOKENS = BATCH * SEQ
+HEAD = D_OUT // 2
+F_PASSES = D_OUT // K_PASS
+
+FLOPS = 2 * 2 * TOKENS * D_IN * D_OUT + 2 * BATCH * SEQ * SEQ * D_OUT
+
+ROUND_TO_INT = 12582912.0
+TWO_PI_HI = 6.28125
+TWO_PI_LO = 2.0 * math.pi - TWO_PI_HI
+
+
+def tile_ropeattention_pa_s_kernel(tc, hidden_states, Wq, bq, Wk, bk, out):
+    nc = tc.nc
+    weights = {"q": Wq, "k": Wk}
+    biases = {"q": bq, "k": bk}
+    sides = ("q", "k")
+
+    with ExitStack() as ctx:
+        keep = ctx.enter_context(tc.tile_pool(name="keep", bufs=1))
+        work = ctx.enter_context(tc.tile_pool(name="work", bufs=2))
+        transposed = ctx.enter_context(tc.psum_pool(name="transposed", bufs=4))
+        projected = ctx.enter_context(tc.psum_pool(name="projected", bufs=3))
+        scores = ctx.enter_context(tc.psum_pool(name="scores", bufs=1))
+
+        x_rows = keep.tile([P, D_IN], BF16)
+        nc.sync.dma_start(out=x_rows[:], in_=hidden_states.rearrange("b s d -> (b s) d"))
+        w_rows = {}
+        for c in range(F_PASSES):
+            for side in sides:
+                w_rows[side, c] = keep.tile([P, PACK, D_IN], BF16, name="w_rows_%s%d" % (side, c))
+                nc.sync.dma_start(
+                    out=w_rows[side, c][:],
+                    in_=weights[side][c * K_PASS : (c + 1) * K_PASS, :].rearrange(
+                        "(p t) d -> p t d", t=PACK
+                    ),
+                )
+        bias_rows = {}
+        for side in sides:
+            bias_rows[side] = keep.tile([P, F_PASSES, PACK], BF16, name="bias_rows_%s" % side)
+            nc.scalar.dma_start(
+                out=bias_rows[side][:],
+                in_=biases[side].rearrange("(c p t) -> p c t", p=P, t=PACK),
+            )
+
+        identity = keep.tile([P, P], F32)
+        make_identity(nc, identity[:])
+
+        exponent = keep.tile([P, F_PASSES], F32)
+        nc.gpsimd.iota(
+            exponent[:],
+            pattern=[[P, F_PASSES]],
+            base=0,
+            channel_multiplier=1,
+            allow_small_or_imprecise_dtypes=True,
+        )
+        nc.gpsimd.tensor_scalar(
+            out=exponent[:], in0=exponent[:], scalar1=-2.0 / HEAD, scalar2=0.0, op0=ALU.mult, op1=ALU.add
+        )
+        ten_thousand = keep.tile([P, F_PASSES], F32)
+        nc.gpsimd.memset(ten_thousand[:], 10000.0)
+        frequency = keep.tile([P, F_PASSES], F32)
+        nc.gpsimd.tensor_tensor(out=frequency[:], in0=ten_thousand[:], in1=exponent[:], op=ALU.pow)
+        position = keep.tile([P, SEQ], F32)
+        nc.gpsimd.iota(
+            position[:], pattern=[[1, SEQ]], base=0, channel_multiplier=0, allow_small_or_imprecise_dtypes=True
+        )
+
+        bias_rot = {}
+        for side in sides:
+            pairs = bias_rows[side][:].rearrange("p c (h e) -> p (c h) e", e=2)
+            bias_rot[side] = keep.tile([P, F_PASSES, PACK], F32, name="bias_rot_%s" % side)
+            rotated = bias_rot[side][:].rearrange("p c (h e) -> p (c h) e", e=2)
+            nc.gpsimd.tensor_tensor(out=rotated[:, :, 0], in0=pairs[:, :, 0], in1=pairs[:, :, 1], op=ALU.subtract)
+            nc.gpsimd.tensor_tensor(out=rotated[:, :, 1], in0=pairs[:, :, 0], in1=pairs[:, :, 1], op=ALU.add)
+
+        angle = keep.tile([P, F_PASSES, 2, SEQ], F32)
+        for c in range(F_PASSES):
+            for h in range(2):
+                nc.vector.tensor_scalar(
+                    out=angle[:, c, h, :],
+                    in0=position[:],
+                    scalar1=frequency[:, c : c + 1],
+                    scalar2=h * math.pi / 2.0,
+                    op0=ALU.mult,
+                    op1=ALU.add,
+                )
+        turns = keep.tile([P, F_PASSES, 2, SEQ], F32)
+        nc.vector.tensor_scalar(
+            out=turns[:], in0=angle[:], scalar1=1.0 / (2.0 * math.pi), scalar2=ROUND_TO_INT, op0=ALU.mult, op1=ALU.add
+        )
+        nc.vector.tensor_scalar(out=turns[:], in0=turns[:], scalar1=ROUND_TO_INT, scalar2=None, op0=ALU.subtract)
+        reduced = keep.tile([P, F_PASSES, 2, SEQ], F32)
+        nc.vector.scalar_tensor_tensor(
+            out=reduced[:].rearrange("p c h s -> p (c h s)"),
+            in0=turns[:].rearrange("p c h s -> p (c h s)"),
+            scalar=-TWO_PI_HI,
+            in1=angle[:].rearrange("p c h s -> p (c h s)"),
+            op0=ALU.mult,
+            op1=ALU.add,
+        )
+        nc.vector.scalar_tensor_tensor(
+            out=reduced[:].rearrange("p c h s -> p (c h s)"),
+            in0=turns[:].rearrange("p c h s -> p (c h s)"),
+            scalar=-TWO_PI_LO,
+            in1=reduced[:].rearrange("p c h s -> p (c h s)"),
+            op0=ALU.mult,
+            op1=ALU.add,
+        )
+        table = keep.tile([P, F_PASSES, 2, SEQ], F32)
+        nc.scalar.activation(out=table[:], in_=reduced[:], func=ACT.Sin)
+
+        x_words = x_rows[:].bitcast(F32)
+        xT = transposed.tile([P, 2, TOKENS], F32, tag="bank")
+        for u in range(2):
+            nc.tensor.transpose(xT[:, u, :], x_words[:, u * P : (u + 1) * P], identity[:])
+        x_grouped = keep.tile([P, 4, TOKENS, PACK], BF16, align_bytes=64)
+        nc.vector.tensor_copy(
+            out=x_grouped[:, 1:4].bitcast(F32),
+            in_=xT[:].rearrange("p u n -> p n u").unsqueeze(1).to_broadcast([P, 3, TOKENS, 2]),
+        )
+        nc.vector.tensor_scalar(
+            out=x_grouped[:, 0].rearrange("p n (u e) -> p n u e", e=2),
+            in0=xT[:].bitcast(BF16).rearrange("p u (n e) -> p n u e", e=2),
+            scalar1=-1.0,
+            scalar2=None,
+            op0=ALU.mult,
+        )
+        x_codes = keep.tile([P, 4 * TOKENS], U32, align_bytes=64)
+        x_scales = keep.tile([P, 4 * TOKENS], U8, align_bytes=64)
+        nc.vector.quantize_mx(
+            out=x_codes[:].bitcast(FP8X4),
+            scales=x_scales[:],
+            in_=x_grouped[:].rearrange("p a n t -> p (a n t)"),
+        )
+        plus_plus = slice(TOKENS, 3 * TOKENS)
+        minus_plus = slice(0, 2 * TOKENS)
+
+        rot_grouped = {}
+        rot_codes = {}
+        rot_scales = {}
+        for side in sides:
+            rot_grouped[side] = keep.tile(
+                [P, F_PASSES, TOKENS, PACK], BF16, name="rot_grouped_%s" % side, align_bytes=64
+            )
+            rot_codes[side] = keep.tile([P, F_PASSES, TOKENS], U32, name="rot_codes_%s" % side, align_bytes=64)
+            rot_scales[side] = keep.tile([P, F_PASSES, TOKENS], U8, name="rot_scales_%s" % side, align_bytes=64)
+        score = scores.tile([P, TOKENS], F32)
+
+        for c in range(F_PASSES):
+            for side in sides:
+                w_words = w_rows[side, c][:].bitcast(F32)
+                w_grouped = work.tile([P, PACK, P, PACK], BF16, align_bytes=64)
+                w_codes = work.tile([P, PACK * P], U32, align_bytes=64)
+                w_scales = work.tile([P, PACK * P], U8, align_bytes=64)
+                for h in range(2):
+                    wT = transposed.tile([P, 2, 2, P], F32, tag="bank")
+                    for e in range(2):
+                        for u in range(2):
+                            nc.tensor.transpose(
+                                wT[:, e, u, :], w_words[:, 2 * h + e, u * P : (u + 1) * P], identity[:]
+                            )
+                    nc.scalar.copy(
+                        out=w_grouped[:, 2 * h : 2 * h + 2].bitcast(F32),
+                        in_=wT[:].rearrange("p e u m -> p e m u"),
+                    )
+                    pair = slice(2 * h * P, (2 * h + 2) * P)
+                    nc.vector.quantize_mx(
+                        out=w_codes[:, pair].bitcast(FP8X4),
+                        scales=w_scales[:, pair],
+                        in_=w_grouped[:, 2 * h : 2 * h + 2].rearrange("p e m t -> p (e m t)"),
+                    )
+
+                y = projected.tile([P, 2, 2, TOKENS], F32)
+                for h in range(2):
+                    for e in range(2):
+                        row = slice((2 * h + e) * P, (2 * h + e + 1) * P)
+                        moving = plus_plus if e == 0 else minus_plus
+                        nc.tensor.matmul_mx(
+                            out=y[:, h].rearrange("p e n -> p (e n)"),
+                            lhsT=w_codes[:, row].bitcast(FP8X4),
+                            lhsT_scale=w_scales[:, row],
+                            rhs=x_codes[:, moving].bitcast(FP8X4),
+                            rhs_scale=x_scales[:, moving],
+                            start=(e == 0),
+                            stop=(e == 1),
+                        )
+
+                biased = work.tile([P, PACK, TOKENS], F32)
+                for t in range(PACK):
+                    nc.scalar.activation(
+                        out=biased[:, t, :],
+                        in_=y[:, t // 2, t % 2, :],
+                        func=ACT.Identity,
+                        bias=bias_rot[side][:, c, t : t + 1],
+                        scale=1.0,
+                    )
+                for b in range(BATCH):
+                    tokens = slice(b * SEQ, (b + 1) * SEQ)
+                    nc.vector.tensor_tensor(
+                        out=rot_grouped[side][:, c, tokens, :].rearrange("p s (h e) -> p s h e", e=2),
+                        in0=biased[:, :, tokens].rearrange("p (h e) s -> p s h e", e=2),
+                        in1=table[:, c].rearrange("p h s -> p s h").unsqueeze(3).to_broadcast([P, SEQ, 2, 2]),
+                        op=ALU.mult,
+                    )
+                nc.vector.quantize_mx(
+                    out=rot_codes[side][:, c, :].bitcast(FP8X4),
+                    scales=rot_scales[side][:, c, :],
+                    in_=rot_grouped[side][:, c].rearrange("p n t -> p (n t)"),
+                )
+
+            nc.tensor.matmul_mx(
+                out=score[:],
+                lhsT=rot_codes["q"][:, c, :].bitcast(FP8X4),
+                lhsT_scale=rot_scales["q"][:, c, :],
+                rhs=rot_codes["k"][:, c, :].bitcast(FP8X4),
+                rhs_scale=rot_scales["k"][:, c, :],
+                start=(c == 0),
+                stop=(c == F_PASSES - 1),
+            )
+
+        scaled = keep.tile([P, SEQ], F32)
+        nc.vector.tensor_scalar(
+            out=scaled[0:SEQ, :], in0=score[0:SEQ, 0:SEQ], scalar1=1.0 / math.sqrt(HEAD), scalar2=None, op0=ALU.mult
+        )
+        nc.scalar.mul(out=scaled[SEQ:P, :], in_=score[SEQ:P, SEQ:P], mul=1.0 / math.sqrt(HEAD))
+        nc.sync.dma_start(out=out.rearrange("b s j -> (b s) j"), in_=scaled[:])

@@ -20,6 +20,8 @@ BATCH, SEQ, D_IN, D_OUT = 2, 64, 512, 1024
 TOKENS = BATCH * SEQ
 HEAD = D_OUT // 2
 F_PASSES = D_OUT // K_PASS
+SIDES = ("q", "k")
+CHUNKS = F_PASSES * len(SIDES)
 
 FLOPS = 2 * 2 * TOKENS * D_IN * D_OUT + 2 * BATCH * SEQ * SEQ * D_OUT
 
@@ -32,38 +34,33 @@ def tile_ropeattention_pa_s_kernel(tc, hidden_states, Wq, bq, Wk, bk, out):
     nc = tc.nc
     weights = {"q": Wq, "k": Wk}
     biases = {"q": bq, "k": bk}
-    sides = ("q", "k")
 
     with ExitStack() as ctx:
+        ctx.enter_context(tc.manual_schedule())
         keep = ctx.enter_context(tc.tile_pool(name="keep", bufs=1))
-        work = ctx.enter_context(tc.tile_pool(name="work", bufs=2))
         transposed = ctx.enter_context(tc.psum_pool(name="transposed", bufs=4))
         projected = ctx.enter_context(tc.psum_pool(name="projected", bufs=3))
         scores = ctx.enter_context(tc.psum_pool(name="scores", bufs=1))
 
-        x_rows = keep.tile([P, D_IN], BF16)
-        nc.sync.dma_start(out=x_rows[:], in_=hidden_states.rearrange("b s d -> (b s) d"))
-        w_rows = {}
-        for c in range(F_PASSES):
-            for side in sides:
-                w_rows[side, c] = keep.tile([P, PACK, D_IN], BF16, name="w_rows_%s%d" % (side, c))
-                nc.sync.dma_start(
-                    out=w_rows[side, c][:],
-                    in_=weights[side][c * K_PASS : (c + 1) * K_PASS, :].rearrange(
-                        "(p t) d -> p t d", t=PACK
-                    ),
-                )
         bias_rows = {}
-        for side in sides:
+        for side in SIDES:
             bias_rows[side] = keep.tile([P, F_PASSES, PACK], BF16, name="bias_rows_%s" % side)
             nc.scalar.dma_start(
                 out=bias_rows[side][:],
                 in_=biases[side].rearrange("(c p t) -> p c t", p=P, t=PACK),
             )
+        x_rows = keep.tile([P, D_IN], BF16)
+        nc.sync.dma_start(out=x_rows[:], in_=hidden_states.rearrange("b s d -> (b s) d"))
+        w_rows = keep.tile([P, CHUNKS, PACK, D_IN], BF16)
+        for i in range(CHUNKS):
+            chunk_rows = weights[SIDES[i % 2]][(i // 2) * K_PASS : (i // 2 + 1) * K_PASS, :].rearrange(
+                "(p t) d -> p t d", t=PACK
+            )
+            for h in range(2):
+                nc.sync.dma_start(out=w_rows[:, i, 2 * h : 2 * h + 2, :], in_=chunk_rows[:, 2 * h : 2 * h + 2, :])
 
-        identity = keep.tile([P, P], F32)
-        make_identity(nc, identity[:])
-
+        ten_thousand = keep.tile([P, F_PASSES], F32)
+        nc.vector.memset(ten_thousand[:], 10000.0)
         exponent = keep.tile([P, F_PASSES], F32)
         nc.gpsimd.iota(
             exponent[:],
@@ -75,17 +72,17 @@ def tile_ropeattention_pa_s_kernel(tc, hidden_states, Wq, bq, Wk, bk, out):
         nc.gpsimd.tensor_scalar(
             out=exponent[:], in0=exponent[:], scalar1=-2.0 / HEAD, scalar2=0.0, op0=ALU.mult, op1=ALU.add
         )
-        ten_thousand = keep.tile([P, F_PASSES], F32)
-        nc.gpsimd.memset(ten_thousand[:], 10000.0)
         frequency = keep.tile([P, F_PASSES], F32)
         nc.gpsimd.tensor_tensor(out=frequency[:], in0=ten_thousand[:], in1=exponent[:], op=ALU.pow)
         position = keep.tile([P, SEQ], F32)
         nc.gpsimd.iota(
             position[:], pattern=[[1, SEQ]], base=0, channel_multiplier=0, allow_small_or_imprecise_dtypes=True
         )
+        identity = keep.tile([P, P], F32)
+        make_identity(nc, identity[:])
 
         bias_rot = {}
-        for side in sides:
+        for side in SIDES:
             pairs = bias_rows[side][:].rearrange("p c (h e) -> p (c h) e", e=2)
             bias_rot[side] = keep.tile([P, F_PASSES, PACK], F32, name="bias_rot_%s" % side)
             rotated = bias_rot[side][:].rearrange("p c (h e) -> p (c h) e", e=2)
@@ -103,6 +100,7 @@ def tile_ropeattention_pa_s_kernel(tc, hidden_states, Wq, bq, Wk, bk, out):
                     op0=ALU.mult,
                     op1=ALU.add,
                 )
+        flat = "p c h s -> p (c h s)"
         turns = keep.tile([P, F_PASSES, 2, SEQ], F32)
         nc.vector.tensor_scalar(
             out=turns[:], in0=angle[:], scalar1=1.0 / (2.0 * math.pi), scalar2=ROUND_TO_INT, op0=ALU.mult, op1=ALU.add
@@ -110,129 +108,126 @@ def tile_ropeattention_pa_s_kernel(tc, hidden_states, Wq, bq, Wk, bk, out):
         nc.vector.tensor_scalar(out=turns[:], in0=turns[:], scalar1=ROUND_TO_INT, scalar2=None, op0=ALU.subtract)
         reduced = keep.tile([P, F_PASSES, 2, SEQ], F32)
         nc.vector.scalar_tensor_tensor(
-            out=reduced[:].rearrange("p c h s -> p (c h s)"),
-            in0=turns[:].rearrange("p c h s -> p (c h s)"),
+            out=reduced[:].rearrange(flat),
+            in0=turns[:].rearrange(flat),
             scalar=-TWO_PI_HI,
-            in1=angle[:].rearrange("p c h s -> p (c h s)"),
+            in1=angle[:].rearrange(flat),
             op0=ALU.mult,
             op1=ALU.add,
         )
         nc.vector.scalar_tensor_tensor(
-            out=reduced[:].rearrange("p c h s -> p (c h s)"),
-            in0=turns[:].rearrange("p c h s -> p (c h s)"),
+            out=reduced[:].rearrange(flat),
+            in0=turns[:].rearrange(flat),
             scalar=-TWO_PI_LO,
-            in1=reduced[:].rearrange("p c h s -> p (c h s)"),
+            in1=reduced[:].rearrange(flat),
             op0=ALU.mult,
             op1=ALU.add,
         )
-        table = keep.tile([P, F_PASSES, 2, SEQ], F32)
-        nc.scalar.activation(out=table[:], in_=reduced[:], func=ACT.Sin)
 
         x_words = x_rows[:].bitcast(F32)
         xT = transposed.tile([P, 2, TOKENS], F32, tag="bank")
         for u in range(2):
             nc.tensor.transpose(xT[:, u, :], x_words[:, u * P : (u + 1) * P], identity[:])
-        x_grouped = keep.tile([P, 4, TOKENS, PACK], BF16, align_bytes=64)
-        nc.vector.tensor_copy(
-            out=x_grouped[:, 1:4].bitcast(F32),
-            in_=xT[:].rearrange("p u n -> p n u").unsqueeze(1).to_broadcast([P, 3, TOKENS, 2]),
+        x_grouped = keep.tile([P, 3, TOKENS, PACK], BF16, align_bytes=64)
+        nc.scalar.copy(
+            out=x_grouped[:, 1:3].bitcast(F32),
+            in_=xT[:].rearrange("p u n -> p n u").unsqueeze(1).to_broadcast([P, 2, TOKENS, 2]),
         )
+        table = keep.tile([P, F_PASSES, 2, SEQ], F32)
+        nc.scalar.activation(out=table[:], in_=reduced[:], func=ACT.Sin)
         nc.vector.tensor_scalar(
-            out=x_grouped[:, 0].rearrange("p n (u e) -> p n u e", e=2),
-            in0=xT[:].bitcast(BF16).rearrange("p u (n e) -> p n u e", e=2),
-            scalar1=-1.0,
-            scalar2=None,
-            op0=ALU.mult,
+            out=x_grouped[:, 0], in0=x_grouped[:, 1], scalar1=-1.0, scalar2=None, op0=ALU.mult
         )
-        x_codes = keep.tile([P, 4 * TOKENS], U32, align_bytes=64)
-        x_scales = keep.tile([P, 4 * TOKENS], U8, align_bytes=64)
-        nc.vector.quantize_mx(
-            out=x_codes[:].bitcast(FP8X4),
-            scales=x_scales[:],
-            in_=x_grouped[:].rearrange("p a n t -> p (a n t)"),
-        )
-        plus_plus = slice(TOKENS, 3 * TOKENS)
+        x_codes = keep.tile([P, 3 * TOKENS], U32, align_bytes=64)
+        x_scales = keep.tile([P, 3 * TOKENS], U8, align_bytes=64)
         minus_plus = slice(0, 2 * TOKENS)
+        plus_plus = slice(TOKENS, 3 * TOKENS)
+        last_copy = slice(2 * TOKENS, 3 * TOKENS)
+        nc.vector.quantize_mx(
+            out=x_codes[:, minus_plus].bitcast(FP8X4),
+            scales=x_scales[:, minus_plus],
+            in_=x_grouped[:, 0:2].rearrange("p a n t -> p (a n t)"),
+        )
+        nc.vector.quantize_mx(
+            out=x_codes[:, last_copy].bitcast(FP8X4),
+            scales=x_scales[:, last_copy],
+            in_=x_grouped[:, 2].rearrange("p n t -> p (n t)"),
+        )
 
-        rot_grouped = {}
-        rot_codes = {}
-        rot_scales = {}
-        for side in sides:
-            rot_grouped[side] = keep.tile(
-                [P, F_PASSES, TOKENS, PACK], BF16, name="rot_grouped_%s" % side, align_bytes=64
-            )
-            rot_codes[side] = keep.tile([P, F_PASSES, TOKENS], U32, name="rot_codes_%s" % side, align_bytes=64)
-            rot_scales[side] = keep.tile([P, F_PASSES, TOKENS], U8, name="rot_scales_%s" % side, align_bytes=64)
+        w_words = w_rows[:].bitcast(F32)
+        w_grouped = keep.tile([P, CHUNKS, PACK, P, PACK], BF16, align_bytes=64)
+        w_codes = keep.tile([P, CHUNKS, PACK, P], U32, align_bytes=64)
+        w_scales = keep.tile([P, CHUNKS, PACK, P], U8, align_bytes=64)
+        rot_planes = keep.tile([P, CHUNKS, PACK, TOKENS], BF16)
+        rot_grouped = keep.tile([P, CHUNKS, TOKENS, PACK], BF16, align_bytes=64)
+        rot_codes = keep.tile([P, CHUNKS, TOKENS], U32, align_bytes=64)
+        rot_scales = keep.tile([P, CHUNKS, TOKENS], U8, align_bytes=64)
         score = scores.tile([P, TOKENS], F32)
 
-        for c in range(F_PASSES):
-            for side in sides:
-                w_words = w_rows[side, c][:].bitcast(F32)
-                w_grouped = work.tile([P, PACK, P, PACK], BF16, align_bytes=64)
-                w_codes = work.tile([P, PACK * P], U32, align_bytes=64)
-                w_scales = work.tile([P, PACK * P], U8, align_bytes=64)
-                for h in range(2):
-                    wT = transposed.tile([P, 2, 2, P], F32, tag="bank")
-                    for e in range(2):
-                        for u in range(2):
-                            nc.tensor.transpose(
-                                wT[:, e, u, :], w_words[:, 2 * h + e, u * P : (u + 1) * P], identity[:]
-                            )
-                    nc.scalar.copy(
-                        out=w_grouped[:, 2 * h : 2 * h + 2].bitcast(F32),
-                        in_=wT[:].rearrange("p e u m -> p e m u"),
-                    )
-                    pair = slice(2 * h * P, (2 * h + 2) * P)
-                    nc.vector.quantize_mx(
-                        out=w_codes[:, pair].bitcast(FP8X4),
-                        scales=w_scales[:, pair],
-                        in_=w_grouped[:, 2 * h : 2 * h + 2].rearrange("p e m t -> p (e m t)"),
-                    )
-
-                y = projected.tile([P, 2, 2, TOKENS], F32)
-                for h in range(2):
-                    for e in range(2):
-                        row = slice((2 * h + e) * P, (2 * h + e + 1) * P)
-                        moving = plus_plus if e == 0 else minus_plus
-                        nc.tensor.matmul_mx(
-                            out=y[:, h].rearrange("p e n -> p (e n)"),
-                            lhsT=w_codes[:, row].bitcast(FP8X4),
-                            lhsT_scale=w_scales[:, row],
-                            rhs=x_codes[:, moving].bitcast(FP8X4),
-                            rhs_scale=x_scales[:, moving],
-                            start=(e == 0),
-                            stop=(e == 1),
+        def quantise_weights(i):
+            for h in range(2):
+                rows = slice(2 * h, 2 * h + 2)
+                wT = transposed.tile([P, 2, 2, P], F32, tag="bank")
+                for e in range(2):
+                    for u in range(2):
+                        nc.tensor.transpose(
+                            wT[:, e, u, :], w_words[:, i, 2 * h + e, u * P : (u + 1) * P], identity[:]
                         )
-
-                biased = work.tile([P, PACK, TOKENS], F32)
-                for t in range(PACK):
-                    nc.scalar.activation(
-                        out=biased[:, t, :],
-                        in_=y[:, t // 2, t % 2, :],
-                        func=ACT.Identity,
-                        bias=bias_rot[side][:, c, t : t + 1],
-                        scale=1.0,
-                    )
-                for b in range(BATCH):
-                    tokens = slice(b * SEQ, (b + 1) * SEQ)
-                    nc.vector.tensor_tensor(
-                        out=rot_grouped[side][:, c, tokens, :].rearrange("p s (h e) -> p s h e", e=2),
-                        in0=biased[:, :, tokens].rearrange("p (h e) s -> p s h e", e=2),
-                        in1=table[:, c].rearrange("p h s -> p s h").unsqueeze(3).to_broadcast([P, SEQ, 2, 2]),
-                        op=ALU.mult,
-                    )
+                nc.scalar.copy(out=w_grouped[:, i, rows].bitcast(F32), in_=wT[:].rearrange("p e u m -> p e m u"))
                 nc.vector.quantize_mx(
-                    out=rot_codes[side][:, c, :].bitcast(FP8X4),
-                    scales=rot_scales[side][:, c, :],
-                    in_=rot_grouped[side][:, c].rearrange("p n t -> p (n t)"),
+                    out=w_codes[:, i, rows].rearrange("p e m -> p (e m)").bitcast(FP8X4),
+                    scales=w_scales[:, i, rows].rearrange("p e m -> p (e m)"),
+                    in_=w_grouped[:, i, rows].rearrange("p e m t -> p (e m t)"),
                 )
 
+        def project_and_rotate(i):
+            y = projected.tile([P, PACK, TOKENS], F32)
+            for t in range(PACK):
+                moving = plus_plus if t % 2 == 0 else minus_plus
+                nc.tensor.matmul_mx(
+                    out=y[:, t - t % 2 : t - t % 2 + 2, :].rearrange("p e n -> p (e n)"),
+                    lhsT=w_codes[:, i, t, :].bitcast(FP8X4),
+                    lhsT_scale=w_scales[:, i, t, :],
+                    rhs=x_codes[:, moving].bitcast(FP8X4),
+                    rhs_scale=x_scales[:, moving],
+                    start=(t % 2 == 0),
+                    stop=(t % 2 == 1),
+                )
+            for t in range(PACK):
+                nc.vector.scalar_tensor_tensor(
+                    out=rot_planes[:, i, t, :].rearrange("p (b s) -> p b s", b=BATCH),
+                    in0=y[:, t, :].rearrange("p (b s) -> p b s", b=BATCH),
+                    scalar=bias_rot[SIDES[i % 2]][:, i // 2, t : t + 1],
+                    in1=table[:, i // 2, t // 2, :].unsqueeze(1).to_broadcast([P, BATCH, SEQ]),
+                    op0=ALU.add,
+                    op1=ALU.mult,
+                )
+
+        def quantise_rotated(i):
+            nc.scalar.copy(out=rot_grouped[:, i], in_=rot_planes[:, i].rearrange("p t n -> p n t"))
+            nc.vector.quantize_mx(
+                out=rot_codes[:, i, :].bitcast(FP8X4),
+                scales=rot_scales[:, i, :],
+                in_=rot_grouped[:, i].rearrange("p n t -> p (n t)"),
+            )
+
+        quantise_weights(0)
+        quantise_weights(1)
+        for i in range(CHUNKS):
+            project_and_rotate(i)
+            if i >= 1:
+                quantise_rotated(i - 1)
+            if i + 2 < CHUNKS:
+                quantise_weights(i + 2)
+        quantise_rotated(CHUNKS - 1)
+
+        for c in range(F_PASSES):
             nc.tensor.matmul_mx(
                 out=score[:],
-                lhsT=rot_codes["q"][:, c, :].bitcast(FP8X4),
-                lhsT_scale=rot_scales["q"][:, c, :],
-                rhs=rot_codes["k"][:, c, :].bitcast(FP8X4),
-                rhs_scale=rot_scales["k"][:, c, :],
+                lhsT=rot_codes[:, 2 * c, :].bitcast(FP8X4),
+                lhsT_scale=rot_scales[:, 2 * c, :],
+                rhs=rot_codes[:, 2 * c + 1, :].bitcast(FP8X4),
+                rhs_scale=rot_scales[:, 2 * c + 1, :],
                 start=(c == 0),
                 stop=(c == F_PASSES - 1),
             )

@@ -8,6 +8,7 @@ F32 = mybir.dt.float32
 BF16 = mybir.dt.bfloat16
 U32 = mybir.dt.uint32
 U8 = mybir.dt.uint8
+I32 = mybir.dt.int32
 FP8X4 = mybir.dt.float8_e4m3fn_x4
 ALU = mybir.AluOpType
 ACT = mybir.ActivationFunctionType
@@ -22,6 +23,9 @@ HEAD = D_OUT // 2
 F_PASSES = D_OUT // K_PASS
 SIDES = ("q", "k")
 CHUNKS = F_PASSES * len(SIDES)
+
+WARM_PASSES = 14
+FILL_PASSES = 3
 
 FLOPS = 2 * 2 * TOKENS * D_IN * D_OUT + 2 * BATCH * SEQ * SEQ * D_OUT
 
@@ -58,6 +62,31 @@ def tile_ropeattention_pa_s_kernel(tc, hidden_states, Wq, bq, Wk, bk, out):
             )
             for h in range(2):
                 nc.sync.dma_start(out=w_rows[:, i, 2 * h : 2 * h + 2, :], in_=chunk_rows[:, 2 * h : 2 * h + 2, :])
+
+        score = scores.tile([P, TOKENS], F32)
+        idle_grouped = keep.tile([P, TOKENS, PACK], BF16, align_bytes=64)
+        idle_codes = keep.tile([P, TOKENS], U32, align_bytes=64)
+        idle_scales = keep.tile([P, TOKENS], U8, align_bytes=64)
+        nc.vector.memset(idle_grouped[:].bitcast(I32), 0)
+        nc.vector.quantize_mx(
+            out=idle_codes[:].bitcast(FP8X4),
+            scales=idle_scales[:],
+            in_=idle_grouped[:].rearrange("p n t -> p (n t)"),
+        )
+
+        def idle_passes(count):
+            for n in range(count):
+                nc.tensor.matmul_mx(
+                    out=score[:],
+                    lhsT=idle_codes[:].bitcast(FP8X4),
+                    lhsT_scale=idle_scales[:],
+                    rhs=idle_codes[:].bitcast(FP8X4),
+                    rhs_scale=idle_scales[:],
+                    start=True,
+                    stop=True,
+                )
+
+        idle_passes(WARM_PASSES)
 
         ten_thousand = keep.tile([P, F_PASSES], F32)
         nc.vector.memset(ten_thousand[:], 10000.0)
@@ -162,9 +191,8 @@ def tile_ropeattention_pa_s_kernel(tc, hidden_states, Wq, bq, Wk, bk, out):
         rot_grouped = keep.tile([P, CHUNKS, TOKENS, PACK], BF16, align_bytes=64)
         rot_codes = keep.tile([P, CHUNKS, TOKENS], U32, align_bytes=64)
         rot_scales = keep.tile([P, CHUNKS, TOKENS], U8, align_bytes=64)
-        score = scores.tile([P, TOKENS], F32)
 
-        def quantise_weights(i):
+        def quantise_weights(i, fill):
             for h in range(2):
                 rows = slice(2 * h, 2 * h + 2)
                 wT = transposed.tile([P, 2, 2, P], F32, tag="bank")
@@ -173,6 +201,7 @@ def tile_ropeattention_pa_s_kernel(tc, hidden_states, Wq, bq, Wk, bk, out):
                         nc.tensor.transpose(
                             wT[:, e, u, :], w_words[:, i, 2 * h + e, u * P : (u + 1) * P], identity[:]
                         )
+                idle_passes(fill)
                 nc.scalar.copy(out=w_grouped[:, i, rows].bitcast(F32), in_=wT[:].rearrange("p e u m -> p e m u"))
                 nc.vector.quantize_mx(
                     out=w_codes[:, i, rows].rearrange("p e m -> p (e m)").bitcast(FP8X4),
@@ -211,14 +240,14 @@ def tile_ropeattention_pa_s_kernel(tc, hidden_states, Wq, bq, Wk, bk, out):
                 in_=rot_grouped[:, i].rearrange("p n t -> p (n t)"),
             )
 
-        quantise_weights(0)
-        quantise_weights(1)
+        quantise_weights(0, FILL_PASSES)
+        quantise_weights(1, FILL_PASSES)
         for i in range(CHUNKS):
             project_and_rotate(i)
             if i >= 1:
                 quantise_rotated(i - 1)
             if i + 2 < CHUNKS:
-                quantise_weights(i + 2)
+                quantise_weights(i + 2, 0)
         quantise_rotated(CHUNKS - 1)
 
         for c in range(F_PASSES):

@@ -25,7 +25,7 @@ SIDES = ("q", "k")
 CHUNKS = F_PASSES * len(SIDES)
 
 WARM_PASSES = 14
-FILL_PASSES = 3
+LEAD = 3
 
 FLOPS = 2 * 2 * TOKENS * D_IN * D_OUT + 2 * BATCH * SEQ * SEQ * D_OUT
 
@@ -74,19 +74,16 @@ def tile_ropeattention_pa_s_kernel(tc, hidden_states, Wq, bq, Wk, bk, out):
             in_=idle_grouped[:].rearrange("p n t -> p (n t)"),
         )
 
-        def idle_passes(count):
-            for n in range(count):
-                nc.tensor.matmul_mx(
-                    out=score[:],
-                    lhsT=idle_codes[:].bitcast(FP8X4),
-                    lhsT_scale=idle_scales[:],
-                    rhs=idle_codes[:].bitcast(FP8X4),
-                    rhs_scale=idle_scales[:],
-                    start=True,
-                    stop=True,
-                )
-
-        idle_passes(WARM_PASSES)
+        for n in range(WARM_PASSES):
+            nc.tensor.matmul_mx(
+                out=score[:],
+                lhsT=idle_codes[:].bitcast(FP8X4),
+                lhsT_scale=idle_scales[:],
+                rhs=idle_codes[:].bitcast(FP8X4),
+                rhs_scale=idle_scales[:],
+                start=True,
+                stop=True,
+            )
 
         ten_thousand = keep.tile([P, F_PASSES], F32)
         nc.vector.memset(ten_thousand[:], 10000.0)
@@ -158,7 +155,7 @@ def tile_ropeattention_pa_s_kernel(tc, hidden_states, Wq, bq, Wk, bk, out):
         for u in range(2):
             nc.tensor.transpose(xT[:, u, :], x_words[:, u * P : (u + 1) * P], identity[:])
         x_grouped = keep.tile([P, 3, TOKENS, PACK], BF16, align_bytes=64)
-        nc.scalar.copy(
+        nc.vector.tensor_copy(
             out=x_grouped[:, 1:3].bitcast(F32),
             in_=xT[:].rearrange("p u n -> p n u").unsqueeze(1).to_broadcast([P, 2, TOKENS, 2]),
         )
@@ -192,7 +189,7 @@ def tile_ropeattention_pa_s_kernel(tc, hidden_states, Wq, bq, Wk, bk, out):
         rot_codes = keep.tile([P, CHUNKS, TOKENS], U32, align_bytes=64)
         rot_scales = keep.tile([P, CHUNKS, TOKENS], U8, align_bytes=64)
 
-        def quantise_weights(i, fill):
+        def quantise_weights(i):
             for h in range(2):
                 rows = slice(2 * h, 2 * h + 2)
                 wT = transposed.tile([P, 2, 2, P], F32, tag="bank")
@@ -201,7 +198,6 @@ def tile_ropeattention_pa_s_kernel(tc, hidden_states, Wq, bq, Wk, bk, out):
                         nc.tensor.transpose(
                             wT[:, e, u, :], w_words[:, i, 2 * h + e, u * P : (u + 1) * P], identity[:]
                         )
-                idle_passes(fill)
                 nc.scalar.copy(out=w_grouped[:, i, rows].bitcast(F32), in_=wT[:].rearrange("p e u m -> p e m u"))
                 nc.vector.quantize_mx(
                     out=w_codes[:, i, rows].rearrange("p e m -> p (e m)").bitcast(FP8X4),
@@ -233,21 +229,22 @@ def tile_ropeattention_pa_s_kernel(tc, hidden_states, Wq, bq, Wk, bk, out):
                 )
 
         def quantise_rotated(i):
-            nc.scalar.copy(out=rot_grouped[:, i], in_=rot_planes[:, i].rearrange("p t n -> p n t"))
+            regroup = nc.vector.tensor_copy if i == CHUNKS - 1 else nc.scalar.copy
+            regroup(out=rot_grouped[:, i], in_=rot_planes[:, i].rearrange("p t n -> p n t"))
             nc.vector.quantize_mx(
                 out=rot_codes[:, i, :].bitcast(FP8X4),
                 scales=rot_scales[:, i, :],
                 in_=rot_grouped[:, i].rearrange("p n t -> p (n t)"),
             )
 
-        quantise_weights(0, FILL_PASSES)
-        quantise_weights(1, FILL_PASSES)
+        for i in range(LEAD):
+            quantise_weights(i)
         for i in range(CHUNKS):
             project_and_rotate(i)
             if i >= 1:
                 quantise_rotated(i - 1)
-            if i + 2 < CHUNKS:
-                quantise_weights(i + 2, 0)
+            if i + LEAD < CHUNKS:
+                quantise_weights(i + LEAD)
         quantise_rotated(CHUNKS - 1)
 
         for c in range(F_PASSES):

import math
from contextlib import ExitStack

import concourse.mybir as mybir
from concourse.masks import make_identity

F32 = mybir.dt.float32
BF16 = mybir.dt.bfloat16
U32 = mybir.dt.uint32
U8 = mybir.dt.uint8
I32 = mybir.dt.int32
FP8X4 = mybir.dt.float8_e4m3fn_x4
ALU = mybir.AluOpType
ACT = mybir.ActivationFunctionType

P = 128
PACK = 4
K_PASS = P * PACK

BATCH, SEQ, D_IN, D_OUT = 2, 64, 512, 1024
TOKENS = BATCH * SEQ
HEAD = D_OUT // 2
F_PASSES = D_OUT // K_PASS
SIDES = ("q", "k")
CHUNKS = F_PASSES * len(SIDES)

WARM_PASSES = 14
LEAD = 3

FLOPS = 2 * 2 * TOKENS * D_IN * D_OUT + 2 * BATCH * SEQ * SEQ * D_OUT

ROUND_TO_INT = 12582912.0
TWO_PI_HI = 6.28125
TWO_PI_LO = 2.0 * math.pi - TWO_PI_HI


def tile_ropeattention_pa_s_kernel(tc, hidden_states, Wq, bq, Wk, bk, out):
    nc = tc.nc
    weights = {"q": Wq, "k": Wk}
    biases = {"q": bq, "k": bk}

    with ExitStack() as ctx:
        ctx.enter_context(tc.manual_schedule())
        keep = ctx.enter_context(tc.tile_pool(name="keep", bufs=1))
        transposed = ctx.enter_context(tc.psum_pool(name="transposed", bufs=4))
        projected = ctx.enter_context(tc.psum_pool(name="projected", bufs=3))
        scores = ctx.enter_context(tc.psum_pool(name="scores", bufs=1))

        bias_rows = {}
        for side in SIDES:
            bias_rows[side] = keep.tile([P, F_PASSES, PACK], BF16, name="bias_rows_%s" % side)
            nc.scalar.dma_start(
                out=bias_rows[side][:],
                in_=biases[side].rearrange("(c p t) -> p c t", p=P, t=PACK),
            )
        x_rows = keep.tile([P, D_IN], BF16)
        nc.sync.dma_start(out=x_rows[:], in_=hidden_states.rearrange("b s d -> (b s) d"))
        w_rows = keep.tile([P, CHUNKS, PACK, D_IN], BF16)
        for i in range(CHUNKS):
            chunk_rows = weights[SIDES[i % 2]][(i // 2) * K_PASS : (i // 2 + 1) * K_PASS, :].rearrange(
                "(p t) d -> p t d", t=PACK
            )
            for h in range(2):
                nc.sync.dma_start(out=w_rows[:, i, 2 * h : 2 * h + 2, :], in_=chunk_rows[:, 2 * h : 2 * h + 2, :])

        score = scores.tile([P, TOKENS], F32)
        idle_grouped = keep.tile([P, TOKENS, PACK], BF16, align_bytes=64)
        idle_codes = keep.tile([P, TOKENS], U32, align_bytes=64)
        idle_scales = keep.tile([P, TOKENS], U8, align_bytes=64)
        nc.vector.memset(idle_grouped[:].bitcast(I32), 0)
        nc.vector.quantize_mx(
            out=idle_codes[:].bitcast(FP8X4),
            scales=idle_scales[:],
            in_=idle_grouped[:].rearrange("p n t -> p (n t)"),
        )

        for n in range(WARM_PASSES):
            nc.tensor.matmul_mx(
                out=score[:],
                lhsT=idle_codes[:].bitcast(FP8X4),
                lhsT_scale=idle_scales[:],
                rhs=idle_codes[:].bitcast(FP8X4),
                rhs_scale=idle_scales[:],
                start=True,
                stop=True,
            )

        ten_thousand = keep.tile([P, F_PASSES], F32)
        nc.vector.memset(ten_thousand[:], 10000.0)
        exponent = keep.tile([P, F_PASSES], F32)
        nc.gpsimd.iota(
            exponent[:],
            pattern=[[P, F_PASSES]],
            base=0,
            channel_multiplier=1,
            allow_small_or_imprecise_dtypes=True,
        )
        nc.gpsimd.tensor_scalar(
            out=exponent[:], in0=exponent[:], scalar1=-2.0 / HEAD, scalar2=0.0, op0=ALU.mult, op1=ALU.add
        )
        frequency = keep.tile([P, F_PASSES], F32)
        nc.gpsimd.tensor_tensor(out=frequency[:], in0=ten_thousand[:], in1=exponent[:], op=ALU.pow)
        position = keep.tile([P, SEQ], F32)
        nc.gpsimd.iota(
            position[:], pattern=[[1, SEQ]], base=0, channel_multiplier=0, allow_small_or_imprecise_dtypes=True
        )
        identity = keep.tile([P, P], F32)
        make_identity(nc, identity[:])

        bias_rot = {}
        for side in SIDES:
            pairs = bias_rows[side][:].rearrange("p c (h e) -> p (c h) e", e=2)
            bias_rot[side] = keep.tile([P, F_PASSES, PACK], F32, name="bias_rot_%s" % side)
            rotated = bias_rot[side][:].rearrange("p c (h e) -> p (c h) e", e=2)
            nc.gpsimd.tensor_tensor(out=rotated[:, :, 0], in0=pairs[:, :, 0], in1=pairs[:, :, 1], op=ALU.subtract)
            nc.gpsimd.tensor_tensor(out=rotated[:, :, 1], in0=pairs[:, :, 0], in1=pairs[:, :, 1], op=ALU.add)

        angle = keep.tile([P, F_PASSES, 2, SEQ], F32)
        for c in range(F_PASSES):
            for h in range(2):
                nc.vector.tensor_scalar(
                    out=angle[:, c, h, :],
                    in0=position[:],
                    scalar1=frequency[:, c : c + 1],
                    scalar2=h * math.pi / 2.0,
                    op0=ALU.mult,
                    op1=ALU.add,
                )
        flat = "p c h s -> p (c h s)"
        turns = keep.tile([P, F_PASSES, 2, SEQ], F32)
        nc.vector.tensor_scalar(
            out=turns[:], in0=angle[:], scalar1=1.0 / (2.0 * math.pi), scalar2=ROUND_TO_INT, op0=ALU.mult, op1=ALU.add
        )
        nc.vector.tensor_scalar(out=turns[:], in0=turns[:], scalar1=ROUND_TO_INT, scalar2=None, op0=ALU.subtract)
        reduced = keep.tile([P, F_PASSES, 2, SEQ], F32)
        nc.vector.scalar_tensor_tensor(
            out=reduced[:].rearrange(flat),
            in0=turns[:].rearrange(flat),
            scalar=-TWO_PI_HI,
            in1=angle[:].rearrange(flat),
            op0=ALU.mult,
            op1=ALU.add,
        )
        nc.vector.scalar_tensor_tensor(
            out=reduced[:].rearrange(flat),
            in0=turns[:].rearrange(flat),
            scalar=-TWO_PI_LO,
            in1=reduced[:].rearrange(flat),
            op0=ALU.mult,
            op1=ALU.add,
        )

        x_words = x_rows[:].bitcast(F32)
        xT = transposed.tile([P, 2, TOKENS], F32, tag="bank")
        for u in range(2):
            nc.tensor.transpose(xT[:, u, :], x_words[:, u * P : (u + 1) * P], identity[:])
        x_grouped = keep.tile([P, 3, TOKENS, PACK], BF16, align_bytes=64)
        nc.vector.tensor_copy(
            out=x_grouped[:, 1:3].bitcast(F32),
            in_=xT[:].rearrange("p u n -> p n u").unsqueeze(1).to_broadcast([P, 2, TOKENS, 2]),
        )
        table = keep.tile([P, F_PASSES, 2, SEQ], F32)
        nc.scalar.activation(out=table[:], in_=reduced[:], func=ACT.Sin)
        nc.vector.tensor_scalar(
            out=x_grouped[:, 0], in0=x_grouped[:, 1], scalar1=-1.0, scalar2=None, op0=ALU.mult
        )
        x_codes = keep.tile([P, 3 * TOKENS], U32, align_bytes=64)
        x_scales = keep.tile([P, 3 * TOKENS], U8, align_bytes=64)
        minus_plus = slice(0, 2 * TOKENS)
        plus_plus = slice(TOKENS, 3 * TOKENS)
        last_copy = slice(2 * TOKENS, 3 * TOKENS)
        nc.vector.quantize_mx(
            out=x_codes[:, minus_plus].bitcast(FP8X4),
            scales=x_scales[:, minus_plus],
            in_=x_grouped[:, 0:2].rearrange("p a n t -> p (a n t)"),
        )
        nc.vector.quantize_mx(
            out=x_codes[:, last_copy].bitcast(FP8X4),
            scales=x_scales[:, last_copy],
            in_=x_grouped[:, 2].rearrange("p n t -> p (n t)"),
        )

        w_words = w_rows[:].bitcast(F32)
        w_grouped = keep.tile([P, CHUNKS, PACK, P, PACK], BF16, align_bytes=64)
        w_codes = keep.tile([P, CHUNKS, PACK, P], U32, align_bytes=64)
        w_scales = keep.tile([P, CHUNKS, PACK, P], U8, align_bytes=64)
        rot_planes = keep.tile([P, CHUNKS, PACK, TOKENS], BF16)
        rot_grouped = keep.tile([P, CHUNKS, TOKENS, PACK], BF16, align_bytes=64)
        rot_codes = keep.tile([P, CHUNKS, TOKENS], U32, align_bytes=64)
        rot_scales = keep.tile([P, CHUNKS, TOKENS], U8, align_bytes=64)

        def quantise_weights(i):
            for h in range(2):
                rows = slice(2 * h, 2 * h + 2)
                wT = transposed.tile([P, 2, 2, P], F32, tag="bank")
                for e in range(2):
                    for u in range(2):
                        nc.tensor.transpose(
                            wT[:, e, u, :], w_words[:, i, 2 * h + e, u * P : (u + 1) * P], identity[:]
                        )
                nc.scalar.copy(out=w_grouped[:, i, rows].bitcast(F32), in_=wT[:].rearrange("p e u m -> p e m u"))
                nc.vector.quantize_mx(
                    out=w_codes[:, i, rows].rearrange("p e m -> p (e m)").bitcast(FP8X4),
                    scales=w_scales[:, i, rows].rearrange("p e m -> p (e m)"),
                    in_=w_grouped[:, i, rows].rearrange("p e m t -> p (e m t)"),
                )

        def project_and_rotate(i):
            y = projected.tile([P, PACK, TOKENS], F32)
            for t in range(PACK):
                moving = plus_plus if t % 2 == 0 else minus_plus
                nc.tensor.matmul_mx(
                    out=y[:, t - t % 2 : t - t % 2 + 2, :].rearrange("p e n -> p (e n)"),
                    lhsT=w_codes[:, i, t, :].bitcast(FP8X4),
                    lhsT_scale=w_scales[:, i, t, :],
                    rhs=x_codes[:, moving].bitcast(FP8X4),
                    rhs_scale=x_scales[:, moving],
                    start=(t % 2 == 0),
                    stop=(t % 2 == 1),
                )
            for t in range(PACK):
                nc.vector.scalar_tensor_tensor(
                    out=rot_planes[:, i, t, :].rearrange("p (b s) -> p b s", b=BATCH),
                    in0=y[:, t, :].rearrange("p (b s) -> p b s", b=BATCH),
                    scalar=bias_rot[SIDES[i % 2]][:, i // 2, t : t + 1],
                    in1=table[:, i // 2, t // 2, :].unsqueeze(1).to_broadcast([P, BATCH, SEQ]),
                    op0=ALU.add,
                    op1=ALU.mult,
                )

        def quantise_rotated(i):
            regroup = nc.vector.tensor_copy if i == CHUNKS - 1 else nc.scalar.copy
            regroup(out=rot_grouped[:, i], in_=rot_planes[:, i].rearrange("p t n -> p n t"))
            nc.vector.quantize_mx(
                out=rot_codes[:, i, :].bitcast(FP8X4),
                scales=rot_scales[:, i, :],
                in_=rot_grouped[:, i].rearrange("p n t -> p (n t)"),
            )

        for i in range(LEAD):
            quantise_weights(i)
        for i in range(CHUNKS):
            project_and_rotate(i)
            if i >= 1:
                quantise_rotated(i - 1)
            if i + LEAD < CHUNKS:
                quantise_weights(i + LEAD)
        quantise_rotated(CHUNKS - 1)

        for c in range(F_PASSES):
            nc.tensor.matmul_mx(
                out=score[:],
                lhsT=rot_codes[:, 2 * c, :].bitcast(FP8X4),
                lhsT_scale=rot_scales[:, 2 * c, :],
                rhs=rot_codes[:, 2 * c + 1, :].bitcast(FP8X4),
                rhs_scale=rot_scales[:, 2 * c + 1, :],
                start=(c == 0),
                stop=(c == F_PASSES - 1),
            )

        scaled = keep.tile([P, SEQ], F32)
        nc.vector.tensor_scalar(
            out=scaled[0:SEQ, :], in0=score[0:SEQ, 0:SEQ], scalar1=1.0 / math.sqrt(HEAD), scalar2=None, op0=ALU.mult
        )
        nc.scalar.mul(out=scaled[SEQ:P, :], in_=score[SEQ:P, SEQ:P], mul=1.0 / math.sqrt(HEAD))
        nc.sync.dma_start(out=out.rearrange("b s j -> (b s) j"), in_=scaled[:])
